import numpy as np
import ml_dtypes


def mxq(x, axis, fmt="e4m3"):
    dtype, down = {"e4m3": (ml_dtypes.float8_e4m3fn, 7), "e5m2": (ml_dtypes.float8_e5m2, 14)}[fmt]
    v = np.moveaxis(np.asarray(x, np.float32).astype(ml_dtypes.bfloat16).astype(np.float64), axis, -1)
    blocks = v.reshape(v.shape[:-1] + (-1, 32))
    amax = np.abs(blocks).max(-1, keepdims=True)
    byte = np.maximum(np.where(amax > 0, np.frexp(amax)[1] - 1 + 127, 0) - down, 1)
    scale = np.exp2(byte - 127.0)
    codes = (blocks / scale).astype(np.float32).astype(dtype).astype(np.float64)
    return np.moveaxis((codes * scale).reshape(v.shape), -1, axis)


WIDE = False


def mx_kscale(k):
    if not WIDE:
        return np.ones(k)
    levels = np.array([10, -10, 5, -5, 0])
    a = np.random.permutation(np.resize(levels, k // 512 * 4)).reshape(k // 512, 4)
    idx = np.arange(k)
    return np.exp2(a[idx // 512, idx % 128 // 32])


BF16 = ml_dtypes.bfloat16


def bf(x):
    return np.asarray(x, np.float32).astype(BF16)


def f64(x):
    return np.asarray(x).astype(np.float64)


B, H, S, D, W = 1, 2, 2048, 128, 512
NEG = -1e9


def setup_inputs():
    t = mx_kscale(W)
    t = np.roll(t, -np.argmax(t))
    s = np.tile(t, S // W)
    q = np.random.standard_normal((B, H, S, D)) * 2.0
    k = np.random.standard_normal((B, H, S, D))
    v = np.random.standard_normal((B, H, S, D))
    q[..., 0] = 8.0
    k[..., 0] += np.log(s) * np.sqrt(D) / 8.0
    v = v * (s.max() / s)[:, None]
    return {"q": bf(q), "k": bf(k), "v": bf(v), "layer_idx": 1}


def reference(q, k, v, layer_idx):
    q, k = f64(q), f64(k)
    vq = mxq(f64(v), 2, "e4m3")
    out = np.zeros((B, H, S, D))
    for i0 in range(0, S, W):
        i1 = i0 + W
        j0 = 0 if layer_idx % 2 == 0 else max(i0 - W, 0)
        s = q[:, :, i0:i1] @ k[:, :, j0:i1].transpose(0, 1, 3, 2) / np.sqrt(D)
        i = np.arange(i0, i1)[:, None]
        j = np.arange(j0, i1)[None, :]
        mask = j <= i
        if layer_idx % 2 != 0:
            mask = mask & (j > i - W)
        s = np.where(mask, s, NEG)
        e = np.exp(s - s.max(-1, keepdims=True))
        out[:, :, i0:i1] = (mxq(e, 3, "e4m3") @ vq[:, :, j0:i1]) / e.sum(-1, keepdims=True)
    return out

@@ -1,0 +1,296 @@
+from contextlib import ExitStack
+import math
+
+import concourse.mybir as mybir
+from concourse.masks import make_identity
+
+F32 = mybir.dt.float32
+BF16 = mybir.dt.bfloat16
+U32 = mybir.dt.uint32
+U8 = mybir.dt.uint8
+FP8X4 = mybir.dt.float8_e4m3fn_x4
+ALU = mybir.AluOpType
+ACT = mybir.ActivationFunctionType
+AX = mybir.AxisListType
+
+H, S, D, W = 2, 2048, 128, 512
+P = 128
+NT = S // P
+TPC = W // P
+NCH = S // W
+NQ = H * NT
+SCALE = 1.0 / math.sqrt(D)
+NEG = -17179869184.0
+FLOPS = 2 * 2 * H * D * (W * W + (NCH - 1) * W * 2 * W)
+
+MANUAL = False
+ROUTE = "G"
+OUT_ENGINE = "S"
+PREP_ENGINE = "V"
+LEAD = 0
+
+
+def tile_multiheadattn_kernel(tc, q, k, v, layer_idx, out):
+    assert layer_idx % 2 == 1
+    nc = tc.nc
+    qv = q.rearrange("b h (n p) d -> (b h) p n d", p=P)
+    kv = k.rearrange("b h (n p) d -> (b h) p n d", p=P)
+    vv = v.rearrange("b h (n p) d -> (b h) p n d", p=P)
+    ov = out.rearrange("b h (n p) d -> (b h) p n d", p=P)
+
+    seq = list(range(NT)) + list(range(NQ - 1, NT - 1, -1))
+    chunks = [(0, c) for c in range(NCH)] + [(1, c) for c in range(NCH - 1, -1, -1)]
+
+    with ExitStack() as ctx:
+        keep = ctx.enter_context(tc.tile_pool(name="keep", bufs=1))
+        small = ctx.enter_context(tc.tile_pool(name="small", bufs=10))
+        epool = ctx.enter_context(tc.tile_pool(name="epool", bufs=3))
+        cpool = ctx.enter_context(tc.tile_pool(name="cpool", bufs=3))
+        opool = ctx.enter_context(tc.tile_pool(name="opool", bufs=4))
+        ps_a = ctx.enter_context(tc.psum_pool(name="ps_a", bufs=3))
+        ps_d = ctx.enter_context(tc.psum_pool(name="ps_d", bufs=2))
+        ps_t = ctx.enter_context(tc.psum_pool(name="ps_t", bufs=2))
+        ps_o = ctx.enter_context(tc.psum_pool(name="ps_o", bufs=1))
+        if MANUAL:
+            ctx.enter_context(tc.manual_schedule())
+
+        q_raw = keep.tile([P, H, NT, D], BF16)
+        k_raw = keep.tile([P, H, NT, D], BF16)
+        v_raw = keep.tile([P, H, NT, D], BF16)
+        qkT = keep.tile([P, H, 2, S], BF16)
+        v_grp = keep.tile([P, H, NCH, D, TPC], BF16, align_bytes=64)
+        v_cod = keep.tile([P, H, NCH * D], U32, align_bytes=64)
+        v_scl = keep.tile([P, H, NCH * D], U8, align_bytes=64)
+        ident = keep.tile([P, P], BF16)
+        mask_f = keep.tile([P, 2, P], F32)
+        mask_b = keep.tile([P, 2, P], BF16)
+        warm = keep.tile([P, 2], F32)
+        ge = []
+        es = []
+        for r in range(TPC):
+            ge_r = keep.tile([P, 2, P, TPC], BF16, name="ge%d" % r, align_bytes=64)
+            ge.append(ge_r)
+            if ROUTE == "G":
+                es_r = keep.tile([P, 2 * TPC, P], BF16, name="es%d" % r)
+                es.append(es_r)
+
+        def load(raw, view, h, c):
+            nc.sync.dma_start(out=raw[:, h, c * TPC:(c + 1) * TPC, :], in_=view[h][:, c * TPC:(c + 1) * TPC, :])
+
+        for x, (h, c) in enumerate(chunks):
+            load(k_raw, kv, h, c)
+            load(q_raw, qv, h, c)
+            if x < H:
+                nc.sync.dma_start(out=v_raw[:, x], in_=vv[x])
+
+        make_identity(nc, ident[:])
+        nc.vector.memset(warm[:, 0:1], 0.0)
+        nc.scalar.activation(out=warm[:, 1:2], in_=warm[:, 0:1], func=ACT.Exp)
+        nc.gpsimd.memset(mask_f[:], 0.0)
+        nc.gpsimd.affine_select(out=mask_f[:, 0, :], in_=mask_f[:, 0, :], compare_op=ALU.is_ge, fill=NEG,
+                                base=0, pattern=[[-1, P]], channel_multiplier=1)
+        nc.gpsimd.affine_select(out=mask_f[:, 1, :], in_=mask_f[:, 1, :], compare_op=ALU.is_ge, fill=NEG,
+                                base=-1, pattern=[[1, P]], channel_multiplier=-1)
+        nc.vector.tensor_copy(out=mask_b[:], in_=mask_f[:])
+        for r in range(TPC):
+            if ROUTE == "G":
+                nc.vector.memset(es[r][:], 0.0)
+            else:
+                nc.vector.memset(ge[r][:], 0.0)
+
+        st = {}
+
+        def where(i):
+            h, n = divmod(i, NT)
+            c, r = divmod(n, TPC)
+            lo = max(n - TPC, 0)
+            return h, n, c, r, lo, n - lo
+
+        def prep(h, c):
+            tp = ps_t.tile([P, 2 * TPC, P], BF16, tag="tp")
+            for j in range(TPC):
+                nc.tensor.transpose(tp[:, j, :], q_raw[:, h, c * TPC + j, :], ident[:])
+            for j in range(TPC):
+                nc.tensor.transpose(tp[:, TPC + j, :], k_raw[:, h, c * TPC + j, :], ident[:])
+            dst = qkT[:, h, :, c * W:(c + 1) * W]
+            src = tp[:].rearrange("p (a j) w -> p a (j w)", a=2)
+            if PREP_ENGINE == "V":
+                nc.vector.tensor_copy(out=dst, in_=src)
+            else:
+                nc.scalar.copy(out=dst, in_=src)
+
+        def vprep(h):
+            nc.gpsimd.tensor_scalar(out=v_grp[:, h], in0=v_raw[:, h].rearrange("p (g t) d -> p g d t", t=TPC),
+                                    scalar1=1.0, scalar2=0.0, op0=ALU.mult, op1=ALU.add)
+            nc.vector.quantize_mx(out=v_cod[:, h, :].bitcast(FP8X4), scales=v_scl[:, h, :],
+                                  in_=v_grp[:, h].rearrange("p g d t -> p (g d t)"))
+
+        def diag_pe(h, c):
+            dg = ps_d.tile([P, TPC, P], F32)
+            st["dg", h, c] = dg
+            for r in range(TPC):
+                n = c * TPC + r
+                nc.tensor.matmul(dg[:, r, :], lhsT=ident[:], rhs=mask_b[:, 0, :], start=True, stop=False)
+                nc.tensor.matmul(dg[:, r, :], lhsT=qkT[:, h, 0, n * P:(n + 1) * P],
+                                 rhs=qkT[:, h, 1, n * P:(n + 1) * P], start=False, stop=True)
+
+        def diag_max(h, c):
+            rd = small.tile([P, TPC], F32)
+            st["rd", h, c] = rd
+            nc.vector.tensor_reduce(out=rd[:], in_=st["dg", h, c][:], axis=AX.X, op=ALU.max)
+
+        def score(i):
+            h, n, c, r, lo, noff = where(i)
+            if noff == 0:
+                return
+            q_t = qkT[:, h, 0, n * P:(n + 1) * P]
+            sa = ps_a.tile([P, W], F32)
+            st["sa", i] = sa
+            first = 0
+            if n >= TPC:
+                nc.tensor.matmul(sa[:, 0:P], lhsT=ident[:], rhs=mask_b[:, 1, :], start=True, stop=False)
+                nc.tensor.matmul(sa[:, 0:P], lhsT=q_t, rhs=qkT[:, h, 1, lo * P:(lo + 1) * P], start=False, stop=True)
+                first = 1
+            nc.tensor.matmul(sa[:, first * P:noff * P], lhsT=q_t, rhs=qkT[:, h, 1, (lo + first) * P:n * P],
+                             start=True, stop=True)
+
+        def rowmax(i):
+            h, n, c, r, lo, noff = where(i)
+            rd = st["rd", h, c]
+            nb = small.tile([P, 1], F32)
+            st["nb", i] = nb
+            if noff == 0:
+                nc.vector.tensor_scalar(out=nb[:], in0=rd[:, r:r + 1], scalar1=-SCALE, scalar2=None, op0=ALU.mult)
+                return
+            r1 = small.tile([P, 1], F32)
+            nc.vector.tensor_reduce(out=r1[:], in_=st["sa", i][:, 0:noff * P], axis=AX.X, op=ALU.max)
+            nc.vector.tensor_scalar(out=nb[:], in0=r1[:], scalar1=rd[:, r:r + 1], scalar2=-SCALE,
+                                    op0=ALU.max, op1=ALU.mult)
+
+        def expo(i):
+            h, n, c, r, lo, noff = where(i)
+            e = epool.tile([P, (TPC + 1) * P], BF16)
+            rs = small.tile([P, 2], F32)
+            st["e", i] = e
+            st["rs", i] = rs
+            nb = st["nb", i]
+            if noff:
+                nc.scalar.activation(out=e[:, 0:noff * P], in_=st["sa", i][:, 0:noff * P], func=ACT.Exp,
+                                     bias=nb[:], scale=SCALE, accum_out=rs[:, 0:1])
+            nc.scalar.activation(out=e[:, noff * P:(noff + 1) * P], in_=st["dg", h, c][:, r, :], func=ACT.Exp,
+                                 bias=nb[:], scale=SCALE, accum_out=rs[:, 1:2])
+
+        def trans(i):
+            h, n, c, r, lo, noff = where(i)
+            et = ps_t.tile([P, 2 * TPC, P], BF16, tag="tp")
+            st["et", i] = et
+            e = st["e", i]
+            for j in range(noff + 1):
+                nc.tensor.transpose(et[:, j, :], e[:, j * P:(j + 1) * P], ident[:])
+
+        def evac(i):
+            h, n, c, r, lo, noff = where(i)
+            et = st["et", i]
+            u0 = lo - c * TPC + TPC
+            nt = noff + 1
+            a0 = u0 // TPC
+            if ROUTE == "G":
+                nc.scalar.copy(out=es[r][:, u0:u0 + nt, :], in_=et[:, 0:nt, :])
+                return
+            for a in range(a0, 2):
+                u_lo = max(u0, a * TPC)
+                u_hi = min(u0 + nt, (a + 1) * TPC)
+                dst = ge[r][:, a, :, u_lo - a * TPC:u_hi - a * TPC]
+                src = et[:, u_lo - u0:u_hi - u0, :].rearrange("p t w -> p w t")
+                if ROUTE == "S":
+                    nc.scalar.copy(out=dst, in_=src)
+                else:
+                    nc.vector.tensor_copy(out=dst, in_=src)
+
+        def regroup(i):
+            h, n, c, r, lo, noff = where(i)
+            a0 = 0 if n >= TPC else 1
+            if ROUTE == "G":
+                nc.gpsimd.tensor_scalar(out=ge[r][:, a0:2], in0=es[r][:, a0 * TPC:2 * TPC, :].rearrange(
+                    "p (a t) w -> p a w t", t=TPC), scalar1=1.0, scalar2=0.0, op0=ALU.mult, op1=ALU.add)
+
+        def quant(i):
+            h, n, c, r, lo, noff = where(i)
+            a0 = 0 if n >= TPC else 1
+            cod = cpool.tile([P, 2 * P], U32, align_bytes=64)
+            scl = cpool.tile([P, 2 * P], U8, align_bytes=64)
+            st["cod", i] = cod
+            st["scl", i] = scl
+            nc.vector.quantize_mx(out=cod[:, a0 * P:2 * P].bitcast(FP8X4), scales=scl[:, a0 * P:2 * P],
+                                  in_=ge[r][:, a0:2].rearrange("p a w t -> p (a w t)"))
+            rs = st["rs", i]
+            rcp = small.tile([P, 1], F32)
+            st["rcp", i] = rcp
+            if noff:
+                rsum = small.tile([P, 1], F32)
+                nc.vector.tensor_scalar(out=rsum[:], in0=rs[:, 0:1], scalar1=rs[:, 1:2], scalar2=None, op0=ALU.add)
+                nc.vector.reciprocal(rcp[:], rsum[:])
+            else:
+                nc.vector.reciprocal(rcp[:], rs[:, 1:2])
+
+        def pv(i):
+            h, n, c, r, lo, noff = where(i)
+            a0 = 0 if n >= TPC else 1
+            acc = ps_o.tile([P, D], F32)
+            st["acc", i] = acc
+            cod = st["cod", i]
+            scl = st["scl", i]
+            for a in range(a0, 2):
+                g = c - 1 + a
+                nc.tensor.matmul_mx(out=acc[:], lhsT=cod[:, a * P:(a + 1) * P].bitcast(FP8X4),
+                                    lhsT_scale=scl[:, a * P:(a + 1) * P],
+                                    rhs=v_cod[:, h, g * D:(g + 1) * D].bitcast(FP8X4),
+                                    rhs_scale=v_scl[:, h, g * D:(g + 1) * D],
+                                    start=(a == a0), stop=(a == 1))
+
+        def finish(i):
+            h, n, c, r, lo, noff = where(i)
+            rcp = st["rcp", i]
+            osb = opool.tile([P, D], F32)
+            if OUT_ENGINE == "V":
+                nc.vector.tensor_scalar(out=osb[:], in0=st["acc", i][:], scalar1=rcp[:], scalar2=None, op0=ALU.mult)
+            else:
+                nc.scalar.activation(out=osb[:], in_=st["acc", i][:], func=ACT.Copy, scale=rcp[:])
+            nc.sync.dma_start(out=ov[h][:, n, :], in_=osb[:])
+
+        prepped = set()
+
+        def prep_for(x):
+            h, c = chunks[x]
+            for cc in (c, c - 1):
+                if cc >= 0 and (h, cc) not in prepped:
+                    prepped.add((h, cc))
+                    prep(h, cc)
+
+        def stage(fn, x):
+            if 0 <= x < NQ:
+                fn(seq[x])
+
+        prep_for(0)
+        diag_pe(0, 0)
+        diag_max(0, 0)
+        vprep(0)
+        vprep(1)
+        for s in range(-LEAD, NQ + 6):
+            sp = s + LEAD
+            stage(pv, s - 5)
+            stage(finish, s - 5)
+            stage(quant, s - 4)
+            stage(regroup, s - 3)
+            stage(trans, s - 2)
+            stage(evac, s - 2)
+            stage(expo, s - 1)
+            stage(score, sp)
+            stage(rowmax, s)
+            nxt = sp // TPC + 1
+            if 0 <= sp and nxt < H * NCH:
+                if sp % TPC == 1:
+                    prep_for(nxt)
+                if sp % TPC == 2:
+                    diag_pe(chunks[nxt][0], chunks[nxt][1])
+                    diag_max(chunks[nxt][0], chunks[nxt][1])

@@ -24,10 +24,11 @@ NEG = -17179869184.0
 FLOPS = 2 * 2 * H * D * (W * W + (NCH - 1) * W * 2 * W)
 
 MANUAL = False
-ROUTE = "G"
-OUT_ENGINE = "S"
+ROUTE = "S"
+OUT_ENGINE = "V"
 PREP_ENGINE = "V"
 LEAD = 0
+QOFF = 4 if ROUTE == "G" else 3
 
 
 def tile_multiheadattn_kernel(tc, q, k, v, layer_idx, out):
@@ -278,9 +279,9 @@ def tile_multiheadattn_kernel(tc, q, k, v, layer_idx, out):
         vprep(1)
         for s in range(-LEAD, NQ + 6):
             sp = s + LEAD
-            stage(pv, s - 5)
-            stage(finish, s - 5)
-            stage(quant, s - 4)
+            stage(pv, s - QOFF - 1)
+            stage(finish, s - QOFF - 1)
+            stage(quant, s - QOFF)
             stage(regroup, s - 3)
             stage(trans, s - 2)
             stage(evac, s - 2)

@@ -23,12 +23,8 @@ SCALE = 1.0 / math.sqrt(D)
 NEG = -17179869184.0
 FLOPS = 2 * 2 * H * D * (W * W + (NCH - 1) * W * 2 * W)
 
-MANUAL = False
-ROUTE = "S"
-OUT_ENGINE = "V"
-PREP_ENGINE = "V"
-LEAD = 0
-QOFF = 4 if ROUTE == "G" else 3
+MANUAL = True
+VLONE = ()
 
 
 def tile_multiheadattn_kernel(tc, q, k, v, layer_idx, out):
@@ -67,13 +63,9 @@ def tile_multiheadattn_kernel(tc, q, k, v, layer_idx, out):
         mask_b = keep.tile([P, 2, P], BF16)
         warm = keep.tile([P, 2], F32)
         ge = []
-        es = []
         for r in range(TPC):
             ge_r = keep.tile([P, 2, P, TPC], BF16, name="ge%d" % r, align_bytes=64)
             ge.append(ge_r)
-            if ROUTE == "G":
-                es_r = keep.tile([P, 2 * TPC, P], BF16, name="es%d" % r)
-                es.append(es_r)
 
         def load(raw, view, h, c):
             nc.sync.dma_start(out=raw[:, h, c * TPC:(c + 1) * TPC, :], in_=view[h][:, c * TPC:(c + 1) * TPC, :])
@@ -92,12 +84,9 @@ def tile_multiheadattn_kernel(tc, q, k, v, layer_idx, out):
                                 base=0, pattern=[[-1, P]], channel_multiplier=1)
         nc.gpsimd.affine_select(out=mask_f[:, 1, :], in_=mask_f[:, 1, :], compare_op=ALU.is_ge, fill=NEG,
                                 base=-1, pattern=[[1, P]], channel_multiplier=-1)
-        nc.vector.tensor_copy(out=mask_b[:], in_=mask_f[:])
         for r in range(TPC):
-            if ROUTE == "G":
-                nc.vector.memset(es[r][:], 0.0)
-            else:
-                nc.vector.memset(ge[r][:], 0.0)
+            nc.vector.memset(ge[r][:], 0.0)
+        nc.vector.tensor_copy(out=mask_b[:], in_=mask_f[:])
 
         st = {}
 
@@ -107,24 +96,26 @@ def tile_multiheadattn_kernel(tc, q, k, v, layer_idx, out):
             lo = max(n - TPC, 0)
             return h, n, c, r, lo, n - lo
 
-        def prep(h, c):
+        def prep_pe(h, c):
             tp = ps_t.tile([P, 2 * TPC, P], BF16, tag="tp")
+            st["tp", h, c] = tp
             for j in range(TPC):
                 nc.tensor.transpose(tp[:, j, :], q_raw[:, h, c * TPC + j, :], ident[:])
             for j in range(TPC):
                 nc.tensor.transpose(tp[:, TPC + j, :], k_raw[:, h, c * TPC + j, :], ident[:])
-            dst = qkT[:, h, :, c * W:(c + 1) * W]
-            src = tp[:].rearrange("p (a j) w -> p a (j w)", a=2)
-            if PREP_ENGINE == "V":
-                nc.vector.tensor_copy(out=dst, in_=src)
-            else:
-                nc.scalar.copy(out=dst, in_=src)
 
-        def vprep(h):
-            nc.gpsimd.tensor_scalar(out=v_grp[:, h], in0=v_raw[:, h].rearrange("p (g t) d -> p g d t", t=TPC),
-                                    scalar1=1.0, scalar2=0.0, op0=ALU.mult, op1=ALU.add)
-            nc.vector.quantize_mx(out=v_cod[:, h, :].bitcast(FP8X4), scales=v_scl[:, h, :],
-                                  in_=v_grp[:, h].rearrange("p g d t -> p (g d t)"))
+        def prep_out(h, c):
+            nc.vector.tensor_copy(out=qkT[:, h, :, c * W:(c + 1) * W],
+                                  in_=st["tp", h, c][:].rearrange("p (a j) w -> p a (j w)", a=2))
+
+        def vprep(h, g):
+            nc.vector.tensor_copy(out=v_grp[:, h, g].rearrange("p (c i) t -> p c t i", i=4),
+                                  in_=v_raw[:, h, g * TPC:(g + 1) * TPC, :].rearrange("p t (c i) -> p c t i", i=4))
+
+        def vquant(h, g):
+            nc.vector.quantize_mx(out=v_cod[:, h, g * D:(g + 1) * D].bitcast(FP8X4),
+                                  scales=v_scl[:, h, g * D:(g + 1) * D],
+                                  in_=v_grp[:, h, g].rearrange("p d t -> p (d t)"))
 
         def diag_pe(h, c):
             dg = ps_d.tile([P, TPC, P], F32)
@@ -140,46 +131,61 @@ def tile_multiheadattn_kernel(tc, q, k, v, layer_idx, out):
             st["rd", h, c] = rd
             nc.vector.tensor_reduce(out=rd[:], in_=st["dg", h, c][:], axis=AX.X, op=ALU.max)
 
-        def score(i):
+        def score_a(i):
             h, n, c, r, lo, noff = where(i)
             if noff == 0:
                 return
-            q_t = qkT[:, h, 0, n * P:(n + 1) * P]
             sa = ps_a.tile([P, W], F32)
             st["sa", i] = sa
-            first = 0
-            if n >= TPC:
-                nc.tensor.matmul(sa[:, 0:P], lhsT=ident[:], rhs=mask_b[:, 1, :], start=True, stop=False)
-                nc.tensor.matmul(sa[:, 0:P], lhsT=q_t, rhs=qkT[:, h, 1, lo * P:(lo + 1) * P], start=False, stop=True)
-                first = 1
-            nc.tensor.matmul(sa[:, first * P:noff * P], lhsT=q_t, rhs=qkT[:, h, 1, (lo + first) * P:n * P],
-                             start=True, stop=True)
+            first = 1 if n >= TPC else 0
+            nc.tensor.matmul(sa[:, first * P:noff * P], lhsT=qkT[:, h, 0, n * P:(n + 1) * P],
+                             rhs=qkT[:, h, 1, (lo + first) * P:n * P], start=True, stop=True)
+
+        def score_b(i):
+            h, n, c, r, lo, noff = where(i)
+            if n < TPC:
+                return
+            sa = st["sa", i]
+            nc.tensor.matmul(sa[:, 0:P], lhsT=ident[:], rhs=mask_b[:, 1, :], start=True, stop=False)
+            nc.tensor.matmul(sa[:, 0:P], lhsT=qkT[:, h, 0, n * P:(n + 1) * P],
+                             rhs=qkT[:, h, 1, lo * P:(lo + 1) * P], start=False, stop=True)
 
         def rowmax(i):
+            h, n, c, r, lo, noff = where(i)
+            if noff == 0:
+                return
+            r1 = small.tile([P, 1], F32)
+            st["r1", i] = r1
+            nc.vector.tensor_reduce(out=r1[:], in_=st["sa", i][:, 0:noff * P], axis=AX.X, op=ALU.max)
+
+        def negmax(i):
             h, n, c, r, lo, noff = where(i)
             rd = st["rd", h, c]
             nb = small.tile([P, 1], F32)
             st["nb", i] = nb
             if noff == 0:
                 nc.vector.tensor_scalar(out=nb[:], in0=rd[:, r:r + 1], scalar1=-SCALE, scalar2=None, op0=ALU.mult)
-                return
-            r1 = small.tile([P, 1], F32)
-            nc.vector.tensor_reduce(out=r1[:], in_=st["sa", i][:, 0:noff * P], axis=AX.X, op=ALU.max)
-            nc.vector.tensor_scalar(out=nb[:], in0=r1[:], scalar1=rd[:, r:r + 1], scalar2=-SCALE,
-                                    op0=ALU.max, op1=ALU.mult)
+            else:
+                nc.vector.tensor_scalar(out=nb[:], in0=st["r1", i][:], scalar1=rd[:, r:r + 1], scalar2=-SCALE,
+                                        op0=ALU.max, op1=ALU.mult)
 
-        def expo(i):
+        def expo(x):
+            i = seq[x]
             h, n, c, r, lo, noff = where(i)
             e = epool.tile([P, (TPC + 1) * P], BF16)
-            rs = small.tile([P, 2], F32)
             st["e", i] = e
-            st["rs", i] = rs
+            if x % 2 == 0:
+                rs = small.tile([P, 2, 2], F32)
+                st["rs", x // 2] = rs
+                if seq[x] % NT == 0 or seq[x + 1] % NT == 0:
+                    nc.vector.memset(rs[:], 0.0)
+            rs = st["rs", x // 2]
             nb = st["nb", i]
             if noff:
                 nc.scalar.activation(out=e[:, 0:noff * P], in_=st["sa", i][:, 0:noff * P], func=ACT.Exp,
-                                     bias=nb[:], scale=SCALE, accum_out=rs[:, 0:1])
+                                     bias=nb[:], scale=SCALE, accum_out=rs[:, x % 2, 0:1])
             nc.scalar.activation(out=e[:, noff * P:(noff + 1) * P], in_=st["dg", h, c][:, r, :], func=ACT.Exp,
-                                 bias=nb[:], scale=SCALE, accum_out=rs[:, 1:2])
+                                 bias=nb[:], scale=SCALE, accum_out=rs[:, x % 2, 1:2])
 
         def trans(i):
             h, n, c, r, lo, noff = where(i)
@@ -189,31 +195,27 @@ def tile_multiheadattn_kernel(tc, q, k, v, layer_idx, out):
             for j in range(noff + 1):
                 nc.tensor.transpose(et[:, j, :], e[:, j * P:(j + 1) * P], ident[:])
 
-        def evac(i):
+        def evac(i, lone):
             h, n, c, r, lo, noff = where(i)
             et = st["et", i]
             u0 = lo - c * TPC + TPC
             nt = noff + 1
-            a0 = u0 // TPC
-            if ROUTE == "G":
-                nc.scalar.copy(out=es[r][:, u0:u0 + nt, :], in_=et[:, 0:nt, :])
-                return
-            for a in range(a0, 2):
+            for a in range(u0 // TPC, 2):
                 u_lo = max(u0, a * TPC)
                 u_hi = min(u0 + nt, (a + 1) * TPC)
                 dst = ge[r][:, a, :, u_lo - a * TPC:u_hi - a * TPC]
                 src = et[:, u_lo - u0:u_hi - u0, :].rearrange("p t w -> p w t")
-                if ROUTE == "S":
+                if r in VLONE and u_hi - u_lo == 1:
+                    if lone:
+                        nc.vector.tensor_copy(out=dst, in_=src)
+                elif not lone:
                     nc.scalar.copy(out=dst, in_=src)
-                else:
-                    nc.vector.tensor_copy(out=dst, in_=src)
 
-        def regroup(i):
-            h, n, c, r, lo, noff = where(i)
-            a0 = 0 if n >= TPC else 1
-            if ROUTE == "G":
-                nc.gpsimd.tensor_scalar(out=ge[r][:, a0:2], in0=es[r][:, a0 * TPC:2 * TPC, :].rearrange(
-                    "p (a t) w -> p a w t", t=TPC), scalar1=1.0, scalar2=0.0, op0=ALU.mult, op1=ALU.add)
+        def evac_s(i):
+            evac(i, False)
+
+        def evac_v(i):
+            evac(i, True)
 
         def quant(i):
             h, n, c, r, lo, noff = where(i)
@@ -224,15 +226,6 @@ def tile_multiheadattn_kernel(tc, q, k, v, layer_idx, out):
             st["scl", i] = scl
             nc.vector.quantize_mx(out=cod[:, a0 * P:2 * P].bitcast(FP8X4), scales=scl[:, a0 * P:2 * P],
                                   in_=ge[r][:, a0:2].rearrange("p a w t -> p (a w t)"))
-            rs = st["rs", i]
-            rcp = small.tile([P, 1], F32)
-            st["rcp", i] = rcp
-            if noff:
-                rsum = small.tile([P, 1], F32)
-                nc.vector.tensor_scalar(out=rsum[:], in0=rs[:, 0:1], scalar1=rs[:, 1:2], scalar2=None, op0=ALU.add)
-                nc.vector.reciprocal(rcp[:], rsum[:])
-            else:
-                nc.vector.reciprocal(rcp[:], rs[:, 1:2])
 
         def pv(i):
             h, n, c, r, lo, noff = where(i)
@@ -249,49 +242,64 @@ def tile_multiheadattn_kernel(tc, q, k, v, layer_idx, out):
                                     rhs_scale=v_scl[:, h, g * D:(g + 1) * D],
                                     start=(a == a0), stop=(a == 1))
 
-        def finish(i):
+        def rsum(x):
+            rsm = small.tile([P, 2], F32)
+            st["rsm", x // 2] = rsm
+            nc.vector.tensor_reduce(out=rsm[:], in_=st["rs", x // 2][:], axis=AX.X, op=ALU.add)
+
+        def recip(x):
+            rcp = small.tile([P, 2], F32)
+            st["rcp", x // 2] = rcp
+            nc.vector.reciprocal(rcp[:], st["rsm", x // 2][:])
+
+        def outp(x):
+            i = seq[x]
             h, n, c, r, lo, noff = where(i)
-            rcp = st["rcp", i]
             osb = opool.tile([P, D], F32)
-            if OUT_ENGINE == "V":
-                nc.vector.tensor_scalar(out=osb[:], in0=st["acc", i][:], scalar1=rcp[:], scalar2=None, op0=ALU.mult)
-            else:
-                nc.scalar.activation(out=osb[:], in_=st["acc", i][:], func=ACT.Copy, scale=rcp[:])
+            nc.vector.tensor_scalar(out=osb[:], in0=st["acc", i][:], scalar1=st["rcp", x // 2][:, x % 2:x % 2 + 1],
+                                    scalar2=None, op0=ALU.mult)
             nc.sync.dma_start(out=ov[h][:, n, :], in_=osb[:])
 
-        prepped = set()
-
-        def prep_for(x):
-            h, c = chunks[x]
-            for cc in (c, c - 1):
-                if cc >= 0 and (h, cc) not in prepped:
-                    prepped.add((h, cc))
-                    prep(h, cc)
 
         def stage(fn, x):
             if 0 <= x < NQ:
                 fn(seq[x])
 
-        prep_for(0)
+        def stage_x(fn, x):
+            if 0 <= x < NQ:
+                fn(x)
+
+        prep_pe(0, 0)
+        prep_out(0, 0)
         diag_pe(0, 0)
         diag_max(0, 0)
-        vprep(0)
-        vprep(1)
-        for s in range(-LEAD, NQ + 6):
-            sp = s + LEAD
-            stage(pv, s - QOFF - 1)
-            stage(finish, s - QOFF - 1)
-            stage(quant, s - QOFF)
-            stage(regroup, s - 3)
-            stage(trans, s - 2)
-            stage(evac, s - 2)
-            stage(expo, s - 1)
-            stage(score, sp)
-            stage(rowmax, s)
-            nxt = sp // TPC + 1
-            if 0 <= sp and nxt < H * NCH:
-                if sp % TPC == 1:
-                    prep_for(nxt)
-                if sp % TPC == 2:
-                    diag_pe(chunks[nxt][0], chunks[nxt][1])
-                    diag_max(chunks[nxt][0], chunks[nxt][1])
+        for s in range(-2, NQ + 4):
+            new_prep = s // 3 + 1 if s >= 0 and s % 3 == 0 and s // 3 + 1 < H * NCH else 0
+            new_diag = s // TPC + 1 if s >= 0 and s % TPC == 1 and s // TPC + 1 < H * NCH else 0
+            stage(trans, s - 1)
+            stage(score_a, s + 2)
+            stage(pv, s - 3)
+            stage(score_b, s + 2)
+            if new_prep:
+                prep_pe(chunks[new_prep][0], chunks[new_prep][1])
+            if new_diag:
+                diag_pe(chunks[new_diag][0], chunks[new_diag][1])
+            if (s - 3) % 2 == 0:
+                stage_x(recip, s - 3)
+            stage(evac_v, s - 2)
+            stage(rowmax, s + 1)
+            stage(quant, s - 2)
+            stage(negmax, s + 1)
+            stage_x(outp, s - 3)
+            if (s - 2) % 2 == 0:
+                stage_x(rsum, s - 2)
+            stage_x(expo, s)
+            stage(evac_s, s - 1)
+            if s >= 0 and s % 2 == 0 and s // 2 < H * NCH:
+                vprep(chunks[s // 2][0], chunks[s // 2][1])
+            if s >= 1 and s % 2 == 1 and s // 2 < H * NCH:
+                vquant(chunks[s // 2][0], chunks[s // 2][1])
+            if new_prep:
+                prep_out(chunks[new_prep][0], chunks[new_prep][1])
+            if new_diag:
+                diag_max(chunks[new_diag][0], chunks[new_diag][1])

@@ -24,7 +24,7 @@ NEG = -17179869184.0
 FLOPS = 2 * 2 * H * D * (W * W + (NCH - 1) * W * 2 * W)
 
 MANUAL = True
-VLONE = ()
+SPREAD = True
 
 
 def tile_multiheadattn_kernel(tc, q, k, v, layer_idx, out):
@@ -62,19 +62,25 @@ def tile_multiheadattn_kernel(tc, q, k, v, layer_idx, out):
         mask_f = keep.tile([P, 2, P], F32)
         mask_b = keep.tile([P, 2, P], BF16)
         warm = keep.tile([P, 2], F32)
+        spread = keep.tile([P, 2, W], BF16)
         ge = []
         for r in range(TPC):
             ge_r = keep.tile([P, 2, P, TPC], BF16, name="ge%d" % r, align_bytes=64)
             ge.append(ge_r)
 
-        def load(raw, view, h, c):
-            nc.sync.dma_start(out=raw[:, h, c * TPC:(c + 1) * TPC, :], in_=view[h][:, c * TPC:(c + 1) * TPC, :])
+        def load(queue, raw, view, h, c):
+            queue.dma_start(out=raw[:, h, c * TPC:(c + 1) * TPC, :], in_=view[h][:, c * TPC:(c + 1) * TPC, :])
 
+        load(nc.sync, k_raw, kv, 0, 0)
+        load(nc.scalar, q_raw, qv, 0, 0)
+        for g in range(NCH):
+            load(nc.sync, v_raw, vv, 0, g)
         for x, (h, c) in enumerate(chunks):
-            load(k_raw, kv, h, c)
-            load(q_raw, qv, h, c)
-            if x < H:
-                nc.sync.dma_start(out=v_raw[:, x], in_=vv[x])
+            if x > 0:
+                load(nc.sync, k_raw, kv, h, c)
+                load(nc.sync, q_raw, qv, h, c)
+            if x == NCH:
+                nc.sync.dma_start(out=v_raw[:, 1], in_=vv[1])
 
         make_identity(nc, ident[:])
         nc.vector.memset(warm[:, 0:1], 0.0)
@@ -87,6 +93,10 @@ def tile_multiheadattn_kernel(tc, q, k, v, layer_idx, out):
         for r in range(TPC):
             nc.vector.memset(ge[r][:], 0.0)
         nc.vector.tensor_copy(out=mask_b[:], in_=mask_f[:])
+        nc.gpsimd.memset(spread[:], 0.0)
+        for y in range(2):
+            nc.gpsimd.affine_select(out=spread[:, y, :], in_=spread[:, y, :], compare_op=ALU.not_equal, fill=1.0,
+                                    base=3 * y, pattern=[[-1, W]], channel_multiplier=TPC)
 
         st = {}
 
@@ -109,8 +119,12 @@ def tile_multiheadattn_kernel(tc, q, k, v, layer_idx, out):
                                   in_=st["tp", h, c][:].rearrange("p (a j) w -> p a (j w)", a=2))
 
         def vprep(h, g):
-            nc.vector.tensor_copy(out=v_grp[:, h, g].rearrange("p (c i) t -> p c t i", i=4),
-                                  in_=v_raw[:, h, g * TPC:(g + 1) * TPC, :].rearrange("p t (c i) -> p c t i", i=4))
+            dst = v_grp[:, h, g].rearrange("p (c i) t -> p c t i", i=4)
+            src = v_raw[:, h, g * TPC:(g + 1) * TPC, :].rearrange("p t (c i) -> p c t i", i=4)
+            if h == 0:
+                nc.scalar.copy(out=dst, in_=src)
+            else:
+                nc.vector.tensor_copy(out=dst, in_=src)
 
         def vquant(h, g):
             nc.vector.quantize_mx(out=v_cod[:, h, g * D:(g + 1) * D].bitcast(FP8X4),
@@ -187,35 +201,42 @@ def tile_multiheadattn_kernel(tc, q, k, v, layer_idx, out):
             nc.scalar.activation(out=e[:, noff * P:(noff + 1) * P], in_=st["dg", h, c][:, r, :], func=ACT.Exp,
                                  bias=nb[:], scale=SCALE, accum_out=rs[:, x % 2, 1:2])
 
-        def trans(i):
+        def passes(i):
             h, n, c, r, lo, noff = where(i)
+            u0 = lo - c * TPC + TPC
+            res = []
+            for a in range(u0 // TPC, 2):
+                u_lo = max(u0, a * TPC)
+                u_hi = min(u0 + noff + 1, (a + 1) * TPC)
+                res.append((a, u_lo - u0, u_hi - u_lo, u_lo - a * TPC))
+            return res
+
+        def trans(i):
             et = ps_t.tile([P, 2 * TPC, P], BF16, tag="tp")
             st["et", i] = et
             e = st["e", i]
-            for j in range(noff + 1):
-                nc.tensor.transpose(et[:, j, :], e[:, j * P:(j + 1) * P], ident[:])
-
-        def evac(i, lone):
-            h, n, c, r, lo, noff = where(i)
-            et = st["et", i]
-            u0 = lo - c * TPC + TPC
-            nt = noff + 1
-            for a in range(u0 // TPC, 2):
-                u_lo = max(u0, a * TPC)
-                u_hi = min(u0 + nt, (a + 1) * TPC)
-                dst = ge[r][:, a, :, u_lo - a * TPC:u_hi - a * TPC]
-                src = et[:, u_lo - u0:u_hi - u0, :].rearrange("p t w -> p w t")
-                if r in VLONE and u_hi - u_lo == 1:
-                    if lone:
-                        nc.vector.tensor_copy(out=dst, in_=src)
-                elif not lone:
-                    nc.scalar.copy(out=dst, in_=src)
+            k = 0
+            for a, j0, cnt, t0 in passes(i):
+                if SPREAD and cnt == 1:
+                    for m in range(TPC):
+                        nc.tensor.transpose(et[:, TPC + m, :], e[:, j0 * P:(j0 + 1) * P],
+                                            spread[:, t0 // 3, m * P:(m + 1) * P])
+                else:
+                    for j in range(j0, j0 + cnt):
+                        nc.tensor.transpose(et[:, k, :], e[:, j * P:(j + 1) * P], ident[:])
+                        k += 1
 
         def evac_s(i):
-            evac(i, False)
-
-        def evac_v(i):
-            evac(i, True)
+            r = i % TPC
+            et = st["et", i]
+            k = 0
+            for a, j0, cnt, t0 in passes(i):
+                if SPREAD and cnt == 1:
+                    nc.scalar.copy(out=ge[r][:, a].rearrange("p w t -> p (w t)"),
+                                   in_=et[:, TPC:2 * TPC, :].rearrange("p t w -> p (t w)"))
+                else:
+                    nc.scalar.copy(out=ge[r][:, a, :, t0:t0 + cnt], in_=et[:, k:k + cnt, :].rearrange("p t w -> p w t"))
+                    k += cnt
 
         def quant(i):
             h, n, c, r, lo, noff = where(i)
@@ -272,7 +293,11 @@ def tile_multiheadattn_kernel(tc, q, k, v, layer_idx, out):
         prep_pe(0, 0)
         prep_out(0, 0)
         diag_pe(0, 0)
+        for g in range(NCH):
+            vprep(0, g)
+        vquant(0, 0)
         diag_max(0, 0)
+        vquant(0, 1)
         for s in range(-2, NQ + 4):
             new_prep = s // 3 + 1 if s >= 0 and s % 3 == 0 and s // 3 + 1 < H * NCH else 0
             new_diag = s // TPC + 1 if s >= 0 and s % TPC == 1 and s // TPC + 1 < H * NCH else 0
@@ -286,7 +311,6 @@ def tile_multiheadattn_kernel(tc, q, k, v, layer_idx, out):
                 diag_pe(chunks[new_diag][0], chunks[new_diag][1])
             if (s - 3) % 2 == 0:
                 stage_x(recip, s - 3)
-            stage(evac_v, s - 2)
             stage(rowmax, s + 1)
             stage(quant, s - 2)
             stage(negmax, s + 1)
@@ -295,9 +319,11 @@ def tile_multiheadattn_kernel(tc, q, k, v, layer_idx, out):
                 stage_x(rsum, s - 2)
             stage_x(expo, s)
             stage(evac_s, s - 1)
-            if s >= 0 and s % 2 == 0 and s // 2 < H * NCH:
+            if 0 <= s < 2:
+                vquant(0, s + 2)
+            if 2 * NCH <= s < 4 * NCH and s % 2 == 0:
                 vprep(chunks[s // 2][0], chunks[s // 2][1])
-            if s >= 1 and s % 2 == 1 and s // 2 < H * NCH:
+            if 2 * NCH <= s < 4 * NCH and s % 2 == 1:
                 vquant(chunks[s // 2][0], chunks[s // 2][1])
             if new_prep:
                 prep_out(chunks[new_prep][0], chunks[new_prep][1])

@@ -147,41 +147,39 @@ def tile_multiheadattn_kernel(tc, q, k, v, layer_idx, out):
 
         def score_a(i):
             h, n, c, r, lo, noff = where(i)
-            if noff == 0:
-                return
             sa = ps_a.tile([P, W], F32)
             st["sa", i] = sa
             first = 1 if n >= TPC else 0
-            nc.tensor.matmul(sa[:, first * P:noff * P], lhsT=qkT[:, h, 0, n * P:(n + 1) * P],
-                             rhs=qkT[:, h, 1, (lo + first) * P:n * P], start=True, stop=True)
+            if noff > first:
+                nc.tensor.matmul(sa[:, first * P:noff * P], lhsT=qkT[:, h, 0, n * P:(n + 1) * P],
+                                 rhs=qkT[:, h, 1, (lo + first) * P:n * P], start=True, stop=True)
 
         def score_b(i):
             h, n, c, r, lo, noff = where(i)
-            if n < TPC:
-                return
             sa = st["sa", i]
-            nc.tensor.matmul(sa[:, 0:P], lhsT=ident[:], rhs=mask_b[:, 1, :], start=True, stop=False)
-            nc.tensor.matmul(sa[:, 0:P], lhsT=qkT[:, h, 0, n * P:(n + 1) * P],
-                             rhs=qkT[:, h, 1, lo * P:(lo + 1) * P], start=False, stop=True)
+            col, key, which = (0, lo, 1) if n >= TPC else (noff, n, 0)
+            nc.tensor.matmul(sa[:, col * P:(col + 1) * P], lhsT=ident[:], rhs=mask_b[:, which, :], start=True, stop=False)
+            nc.tensor.matmul(sa[:, col * P:(col + 1) * P], lhsT=qkT[:, h, 0, n * P:(n + 1) * P],
+                             rhs=qkT[:, h, 1, key * P:(key + 1) * P], start=False, stop=True)
+
+        def width(i):
+            h, n, c, r, lo, noff = where(i)
+            return noff * P if n >= TPC else (noff + 1) * P
 
         def rowmax(i):
-            h, n, c, r, lo, noff = where(i)
-            if noff == 0:
-                return
             r1 = small.tile([P, 1], F32)
             st["r1", i] = r1
-            nc.vector.tensor_reduce(out=r1[:], in_=st["sa", i][:, 0:noff * P], axis=AX.X, op=ALU.max)
+            nc.vector.tensor_reduce(out=r1[:], in_=st["sa", i][:, 0:width(i)], axis=AX.X, op=ALU.max)
 
         def negmax(i):
             h, n, c, r, lo, noff = where(i)
-            rd = st["rd", h, c]
             nb = small.tile([P, 1], F32)
             st["nb", i] = nb
-            if noff == 0:
-                nc.vector.tensor_scalar(out=nb[:], in0=rd[:, r:r + 1], scalar1=-SCALE, scalar2=None, op0=ALU.mult)
+            if n < TPC:
+                nc.vector.tensor_scalar(out=nb[:], in0=st["r1", i][:], scalar1=-SCALE, scalar2=None, op0=ALU.mult)
             else:
-                nc.vector.tensor_scalar(out=nb[:], in0=st["r1", i][:], scalar1=rd[:, r:r + 1], scalar2=-SCALE,
-                                        op0=ALU.max, op1=ALU.mult)
+                nc.vector.tensor_scalar(out=nb[:], in0=st["r1", i][:], scalar1=st["rd", h, c][:, r:r + 1],
+                                        scalar2=-SCALE, op0=ALU.max, op1=ALU.mult)
 
         def expo(x):
             i = seq[x]
@@ -191,15 +189,15 @@ def tile_multiheadattn_kernel(tc, q, k, v, layer_idx, out):
             if x % 2 == 0:
                 rs = small.tile([P, 2, 2], F32)
                 st["rs", x // 2] = rs
-                if seq[x] % NT == 0 or seq[x + 1] % NT == 0:
+                if n < TPC:
                     nc.vector.memset(rs[:], 0.0)
             rs = st["rs", x // 2]
             nb = st["nb", i]
-            if noff:
-                nc.scalar.activation(out=e[:, 0:noff * P], in_=st["sa", i][:, 0:noff * P], func=ACT.Exp,
-                                     bias=nb[:], scale=SCALE, accum_out=rs[:, x % 2, 0:1])
-            nc.scalar.activation(out=e[:, noff * P:(noff + 1) * P], in_=st["dg", h, c][:, r, :], func=ACT.Exp,
-                                 bias=nb[:], scale=SCALE, accum_out=rs[:, x % 2, 1:2])
+            nc.scalar.activation(out=e[:, 0:width(i)], in_=st["sa", i][:, 0:width(i)], func=ACT.Exp,
+                                 bias=nb[:], scale=SCALE, accum_out=rs[:, x % 2, 0:1])
+            if n >= TPC:
+                nc.scalar.activation(out=e[:, noff * P:(noff + 1) * P], in_=st["dg", h, c][:, r, :], func=ACT.Exp,
+                                     bias=nb[:], scale=SCALE, accum_out=rs[:, x % 2, 1:2])
 
         def passes(i):
             h, n, c, r, lo, noff = where(i)
@@ -292,23 +290,21 @@ def tile_multiheadattn_kernel(tc, q, k, v, layer_idx, out):
 
         prep_pe(0, 0)
         prep_out(0, 0)
-        diag_pe(0, 0)
         for g in range(NCH):
             vprep(0, g)
         vquant(0, 0)
-        diag_max(0, 0)
         vquant(0, 1)
         for s in range(-2, NQ + 4):
             new_prep = s // 3 + 1 if s >= 0 and s % 3 == 0 and s // 3 + 1 < H * NCH else 0
-            new_diag = s // TPC + 1 if s >= 0 and s % TPC == 1 and s // TPC + 1 < H * NCH else 0
+            nxt = s // TPC + 1 if s >= 0 and s // TPC + 1 < H * NCH and chunks[s // TPC + 1][1] > 0 else 0
             stage(trans, s - 1)
             stage(score_a, s + 2)
             stage(pv, s - 3)
             stage(score_b, s + 2)
             if new_prep:
                 prep_pe(chunks[new_prep][0], chunks[new_prep][1])
-            if new_diag:
-                diag_pe(chunks[new_diag][0], chunks[new_diag][1])
+            if nxt and s % TPC == 1:
+                diag_pe(chunks[nxt][0], chunks[nxt][1])
             if (s - 3) % 2 == 0:
                 stage_x(recip, s - 3)
             stage(rowmax, s + 1)
@@ -327,5 +323,5 @@ def tile_multiheadattn_kernel(tc, q, k, v, layer_idx, out):
                 vquant(chunks[s // 2][0], chunks[s // 2][1])
             if new_prep:
                 prep_out(chunks[new_prep][0], chunks[new_prep][1])
-            if new_diag:
-                diag_max(chunks[new_diag][0], chunks[new_diag][1])
+            if nxt and s % TPC == 2:
+                diag_max(chunks[nxt][0], chunks[nxt][1])

@@ -189,8 +189,6 @@ def tile_multiheadattn_kernel(tc, q, k, v, layer_idx, out):
             if x % 2 == 0:
                 rs = small.tile([P, 2, 2], F32)
                 st["rs", x // 2] = rs
-                if n < TPC:
-                    nc.vector.memset(rs[:], 0.0)
             rs = st["rs", x // 2]
             nb = st["nb", i]
             nc.scalar.activation(out=e[:, 0:width(i)], in_=st["sa", i][:, 0:width(i)], func=ACT.Exp,
@@ -262,6 +260,8 @@ def tile_multiheadattn_kernel(tc, q, k, v, layer_idx, out):
                                     start=(a == a0), stop=(a == 1))
 
         def rsum(x):
+            if seq[x] % NT < TPC:
+                return
             rsm = small.tile([P, 2], F32)
             st["rsm", x // 2] = rsm
             nc.vector.tensor_reduce(out=rsm[:], in_=st["rs", x // 2][:], axis=AX.X, op=ALU.add)
@@ -269,7 +269,10 @@ def tile_multiheadattn_kernel(tc, q, k, v, layer_idx, out):
         def recip(x):
             rcp = small.tile([P, 2], F32)
             st["rcp", x // 2] = rcp
-            nc.vector.reciprocal(rcp[:], st["rsm", x // 2][:])
+            if seq[x] % NT < TPC:
+                nc.vector.reciprocal(rcp[:], st["rs", x // 2][:, :, 0])
+            else:
+                nc.vector.reciprocal(rcp[:], st["rsm", x // 2][:])
 
         def outp(x):
             i = seq[x]

@@ -20,22 +20,19 @@ TPC = W // P
 NCH = S // W
 NQ = H * NT
 SCALE = 1.0 / math.sqrt(D)
-NEG = -17179869184.0
+MASKED = -17179869184.0
 FLOPS = 2 * 2 * H * D * (W * W + (NCH - 1) * W * 2 * W)
-
-MANUAL = True
-SPREAD = True
 
 
 def tile_multiheadattn_kernel(tc, q, k, v, layer_idx, out):
-    assert layer_idx % 2 == 1
+    assert layer_idx % 2 == 1, "only the local mask of the odd layers is built"
     nc = tc.nc
     qv = q.rearrange("b h (n p) d -> (b h) p n d", p=P)
     kv = k.rearrange("b h (n p) d -> (b h) p n d", p=P)
     vv = v.rearrange("b h (n p) d -> (b h) p n d", p=P)
     ov = out.rearrange("b h (n p) d -> (b h) p n d", p=P)
 
-    seq = list(range(NT)) + list(range(NQ - 1, NT - 1, -1))
+    tiles = [(0, n) for n in range(NT)] + [(1, n) for n in range(NT - 1, -1, -1)]
     chunks = [(0, c) for c in range(NCH)] + [(1, c) for c in range(NCH - 1, -1, -1)]
 
     with ExitStack() as ctx:
@@ -48,8 +45,7 @@ def tile_multiheadattn_kernel(tc, q, k, v, layer_idx, out):
         ps_d = ctx.enter_context(tc.psum_pool(name="ps_d", bufs=2))
         ps_t = ctx.enter_context(tc.psum_pool(name="ps_t", bufs=2))
         ps_o = ctx.enter_context(tc.psum_pool(name="ps_o", bufs=1))
-        if MANUAL:
-            ctx.enter_context(tc.manual_schedule())
+        ctx.enter_context(tc.manual_schedule())
 
         q_raw = keep.tile([P, H, NT, D], BF16)
         k_raw = keep.tile([P, H, NT, D], BF16)
@@ -61,8 +57,9 @@ def tile_multiheadattn_kernel(tc, q, k, v, layer_idx, out):
         ident = keep.tile([P, P], BF16)
         mask_f = keep.tile([P, 2, P], F32)
         mask_b = keep.tile([P, 2, P], BF16)
-        warm = keep.tile([P, 2], F32)
         spread = keep.tile([P, 2, W], BF16)
+        warm = keep.tile([P, 2], F32)
+        rs = keep.tile([P, NQ, 2], F32)
         ge = []
         for r in range(TPC):
             ge_r = keep.tile([P, 2, P, TPC], BF16, name="ge%d" % r, align_bytes=64)
@@ -86,39 +83,34 @@ def tile_multiheadattn_kernel(tc, q, k, v, layer_idx, out):
         nc.vector.memset(warm[:, 0:1], 0.0)
         nc.scalar.activation(out=warm[:, 1:2], in_=warm[:, 0:1], func=ACT.Exp)
         nc.gpsimd.memset(mask_f[:], 0.0)
-        nc.gpsimd.affine_select(out=mask_f[:, 0, :], in_=mask_f[:, 0, :], compare_op=ALU.is_ge, fill=NEG,
+        nc.gpsimd.affine_select(out=mask_f[:, 0, :], in_=mask_f[:, 0, :], compare_op=ALU.is_ge, fill=MASKED,
                                 base=0, pattern=[[-1, P]], channel_multiplier=1)
-        nc.gpsimd.affine_select(out=mask_f[:, 1, :], in_=mask_f[:, 1, :], compare_op=ALU.is_ge, fill=NEG,
+        nc.gpsimd.affine_select(out=mask_f[:, 1, :], in_=mask_f[:, 1, :], compare_op=ALU.is_ge, fill=MASKED,
                                 base=-1, pattern=[[1, P]], channel_multiplier=-1)
-        for r in range(TPC):
+        for r in range(1, TPC - 1):
             nc.vector.memset(ge[r][:], 0.0)
+        nc.vector.memset(rs[:], 0.0)
         nc.vector.tensor_copy(out=mask_b[:], in_=mask_f[:])
         nc.gpsimd.memset(spread[:], 0.0)
         for y in range(2):
             nc.gpsimd.affine_select(out=spread[:, y, :], in_=spread[:, y, :], compare_op=ALU.not_equal, fill=1.0,
                                     base=3 * y, pattern=[[-1, W]], channel_multiplier=TPC)
 
-        st = {}
+        live = {}
 
-        def where(i):
-            h, n = divmod(i, NT)
-            c, r = divmod(n, TPC)
-            lo = max(n - TPC, 0)
-            return h, n, c, r, lo, n - lo
-
-        def prep_pe(h, c):
+        def transpose_qk(h, c):
             tp = ps_t.tile([P, 2 * TPC, P], BF16, tag="tp")
-            st["tp", h, c] = tp
+            live["tp", h, c] = tp
             for j in range(TPC):
                 nc.tensor.transpose(tp[:, j, :], q_raw[:, h, c * TPC + j, :], ident[:])
             for j in range(TPC):
                 nc.tensor.transpose(tp[:, TPC + j, :], k_raw[:, h, c * TPC + j, :], ident[:])
 
-        def prep_out(h, c):
+        def copy_qk(h, c):
             nc.vector.tensor_copy(out=qkT[:, h, :, c * W:(c + 1) * W],
-                                  in_=st["tp", h, c][:].rearrange("p (a j) w -> p a (j w)", a=2))
+                                  in_=live["tp", h, c][:].rearrange("p (a j) w -> p a (j w)", a=2))
 
-        def vprep(h, g):
+        def regroup_v(h, g):
             dst = v_grp[:, h, g].rearrange("p (c i) t -> p c t i", i=4)
             src = v_raw[:, h, g * TPC:(g + 1) * TPC, :].rearrange("p t (c i) -> p c t i", i=4)
             if h == 0:
@@ -126,205 +118,196 @@ def tile_multiheadattn_kernel(tc, q, k, v, layer_idx, out):
             else:
                 nc.vector.tensor_copy(out=dst, in_=src)
 
-        def vquant(h, g):
+        def quantise_v(h, g):
             nc.vector.quantize_mx(out=v_cod[:, h, g * D:(g + 1) * D].bitcast(FP8X4),
                                   scales=v_scl[:, h, g * D:(g + 1) * D],
                                   in_=v_grp[:, h, g].rearrange("p d t -> p (d t)"))
 
-        def diag_pe(h, c):
+        def diagonal_scores(h, c):
             dg = ps_d.tile([P, TPC, P], F32)
-            st["dg", h, c] = dg
+            live["dg", h, c] = dg
             for r in range(TPC):
                 n = c * TPC + r
                 nc.tensor.matmul(dg[:, r, :], lhsT=ident[:], rhs=mask_b[:, 0, :], start=True, stop=False)
                 nc.tensor.matmul(dg[:, r, :], lhsT=qkT[:, h, 0, n * P:(n + 1) * P],
                                  rhs=qkT[:, h, 1, n * P:(n + 1) * P], start=False, stop=True)
 
-        def diag_max(h, c):
+        def diagonal_max(h, c):
             rd = small.tile([P, TPC], F32)
-            st["rd", h, c] = rd
-            nc.vector.tensor_reduce(out=rd[:], in_=st["dg", h, c][:], axis=AX.X, op=ALU.max)
+            live["rd", h, c] = rd
+            nc.vector.tensor_reduce(out=rd[:], in_=live["dg", h, c][:], axis=AX.X, op=ALU.max)
 
-        def score_a(i):
-            h, n, c, r, lo, noff = where(i)
+        def older(n):
+            return min(n, TPC)
+
+        def scores_unmasked(x):
+            h, n = tiles[x]
+            if n == 0:
+                return
             sa = ps_a.tile([P, W], F32)
-            st["sa", i] = sa
+            live["sa", x] = sa
             first = 1 if n >= TPC else 0
-            if noff > first:
-                nc.tensor.matmul(sa[:, first * P:noff * P], lhsT=qkT[:, h, 0, n * P:(n + 1) * P],
-                                 rhs=qkT[:, h, 1, (lo + first) * P:n * P], start=True, stop=True)
+            nc.tensor.matmul(sa[:, first * P:older(n) * P], lhsT=qkT[:, h, 0, n * P:(n + 1) * P],
+                             rhs=qkT[:, h, 1, (n - older(n) + first) * P:n * P], start=True, stop=True)
 
-        def score_b(i):
-            h, n, c, r, lo, noff = where(i)
-            sa = st["sa", i]
-            col, key, which = (0, lo, 1) if n >= TPC else (noff, n, 0)
-            nc.tensor.matmul(sa[:, col * P:(col + 1) * P], lhsT=ident[:], rhs=mask_b[:, which, :], start=True, stop=False)
-            nc.tensor.matmul(sa[:, col * P:(col + 1) * P], lhsT=qkT[:, h, 0, n * P:(n + 1) * P],
-                             rhs=qkT[:, h, 1, key * P:(key + 1) * P], start=False, stop=True)
-
-        def width(i):
-            h, n, c, r, lo, noff = where(i)
-            return noff * P if n >= TPC else (noff + 1) * P
-
-        def rowmax(i):
-            r1 = small.tile([P, 1], F32)
-            st["r1", i] = r1
-            nc.vector.tensor_reduce(out=r1[:], in_=st["sa", i][:, 0:width(i)], axis=AX.X, op=ALU.max)
-
-        def negmax(i):
-            h, n, c, r, lo, noff = where(i)
-            nb = small.tile([P, 1], F32)
-            st["nb", i] = nb
+        def scores_masked(x):
+            h, n = tiles[x]
             if n < TPC:
-                nc.vector.tensor_scalar(out=nb[:], in0=st["r1", i][:], scalar1=-SCALE, scalar2=None, op0=ALU.mult)
+                return
+            sa = live["sa", x]
+            nc.tensor.matmul(sa[:, 0:P], lhsT=ident[:], rhs=mask_b[:, 1, :], start=True, stop=False)
+            nc.tensor.matmul(sa[:, 0:P], lhsT=qkT[:, h, 0, n * P:(n + 1) * P],
+                             rhs=qkT[:, h, 1, (n - TPC) * P:(n - TPC + 1) * P], start=False, stop=True)
+
+        def row_max(x):
+            h, n = tiles[x]
+            if n == 0:
+                return
+            r1 = small.tile([P, 1], F32)
+            live["r1", x] = r1
+            nc.vector.tensor_reduce(out=r1[:], in_=live["sa", x][:, 0:older(n) * P], axis=AX.X, op=ALU.max)
+
+        def bias(x):
+            h, n = tiles[x]
+            rd = live["rd", h, n // TPC]
+            nb = small.tile([P, 1], F32)
+            live["nb", x] = nb
+            if n == 0:
+                nc.vector.tensor_scalar(out=nb[:], in0=rd[:, 0:1], scalar1=-SCALE, scalar2=None, op0=ALU.mult)
             else:
-                nc.vector.tensor_scalar(out=nb[:], in0=st["r1", i][:], scalar1=st["rd", h, c][:, r:r + 1],
+                nc.vector.tensor_scalar(out=nb[:], in0=live["r1", x][:], scalar1=rd[:, n % TPC:n % TPC + 1],
                                         scalar2=-SCALE, op0=ALU.max, op1=ALU.mult)
 
-        def expo(x):
-            i = seq[x]
-            h, n, c, r, lo, noff = where(i)
+        def exponentials(x):
+            h, n = tiles[x]
             e = epool.tile([P, (TPC + 1) * P], BF16)
-            st["e", i] = e
-            if x % 2 == 0:
-                rs = small.tile([P, 2, 2], F32)
-                st["rs", x // 2] = rs
-            rs = st["rs", x // 2]
-            nb = st["nb", i]
-            nc.scalar.activation(out=e[:, 0:width(i)], in_=st["sa", i][:, 0:width(i)], func=ACT.Exp,
-                                 bias=nb[:], scale=SCALE, accum_out=rs[:, x % 2, 0:1])
-            if n >= TPC:
-                nc.scalar.activation(out=e[:, noff * P:(noff + 1) * P], in_=st["dg", h, c][:, r, :], func=ACT.Exp,
-                                     bias=nb[:], scale=SCALE, accum_out=rs[:, x % 2, 1:2])
+            live["e", x] = e
+            nb = live["nb", x]
+            if n > 0:
+                nc.scalar.activation(out=e[:, 0:older(n) * P], in_=live["sa", x][:, 0:older(n) * P], func=ACT.Exp,
+                                     bias=nb[:], scale=SCALE, accum_out=rs[:, x, 0:1])
+            nc.scalar.activation(out=e[:, older(n) * P:(older(n) + 1) * P], in_=live["dg", h, n // TPC][:, n % TPC, :],
+                                 func=ACT.Exp, bias=nb[:], scale=SCALE, accum_out=rs[:, x, 1:2])
 
-        def passes(i):
-            h, n, c, r, lo, noff = where(i)
-            u0 = lo - c * TPC + TPC
-            res = []
+        def passes(n):
+            u0 = n - older(n) - (n // TPC - 1) * TPC
+            found = []
             for a in range(u0 // TPC, 2):
                 u_lo = max(u0, a * TPC)
-                u_hi = min(u0 + noff + 1, (a + 1) * TPC)
-                res.append((a, u_lo - u0, u_hi - u_lo, u_lo - a * TPC))
-            return res
+                u_hi = min(u0 + older(n) + 1, (a + 1) * TPC)
+                found.append((a, u_lo - u0, u_hi - u_lo, u_lo - a * TPC))
+            return found
 
-        def trans(i):
+        def transpose_e(x):
+            h, n = tiles[x]
             et = ps_t.tile([P, 2 * TPC, P], BF16, tag="tp")
-            st["et", i] = et
-            e = st["e", i]
-            k = 0
-            for a, j0, cnt, t0 in passes(i):
-                if SPREAD and cnt == 1:
+            live["et", x] = et
+            e = live["e", x]
+            filled = 0
+            for a, j0, count, t0 in passes(n):
+                if count == 1:
                     for m in range(TPC):
                         nc.tensor.transpose(et[:, TPC + m, :], e[:, j0 * P:(j0 + 1) * P],
                                             spread[:, t0 // 3, m * P:(m + 1) * P])
                 else:
-                    for j in range(j0, j0 + cnt):
-                        nc.tensor.transpose(et[:, k, :], e[:, j * P:(j + 1) * P], ident[:])
-                        k += 1
+                    for j in range(j0, j0 + count):
+                        nc.tensor.transpose(et[:, filled, :], e[:, j * P:(j + 1) * P], ident[:])
+                        filled += 1
 
-        def evac_s(i):
-            r = i % TPC
-            et = st["et", i]
-            k = 0
-            for a, j0, cnt, t0 in passes(i):
-                if SPREAD and cnt == 1:
-                    nc.scalar.copy(out=ge[r][:, a].rearrange("p w t -> p (w t)"),
+        def copy_e(x):
+            h, n = tiles[x]
+            et = live["et", x]
+            done = 0
+            for a, j0, count, t0 in passes(n):
+                if count == 1:
+                    nc.scalar.copy(out=ge[n % TPC][:, a].rearrange("p w t -> p (w t)"),
                                    in_=et[:, TPC:2 * TPC, :].rearrange("p t w -> p (t w)"))
                 else:
-                    nc.scalar.copy(out=ge[r][:, a, :, t0:t0 + cnt], in_=et[:, k:k + cnt, :].rearrange("p t w -> p w t"))
-                    k += cnt
+                    nc.scalar.copy(out=ge[n % TPC][:, a, :, t0:t0 + count],
+                                   in_=et[:, done:done + count, :].rearrange("p t w -> p w t"))
+                    done += count
 
-        def quant(i):
-            h, n, c, r, lo, noff = where(i)
+        def quantise_e(x):
+            h, n = tiles[x]
             a0 = 0 if n >= TPC else 1
             cod = cpool.tile([P, 2 * P], U32, align_bytes=64)
             scl = cpool.tile([P, 2 * P], U8, align_bytes=64)
-            st["cod", i] = cod
-            st["scl", i] = scl
+            live["cod", x] = cod
+            live["scl", x] = scl
             nc.vector.quantize_mx(out=cod[:, a0 * P:2 * P].bitcast(FP8X4), scales=scl[:, a0 * P:2 * P],
-                                  in_=ge[r][:, a0:2].rearrange("p a w t -> p (a w t)"))
+                                  in_=ge[n % TPC][:, a0:2].rearrange("p a w t -> p (a w t)"))
 
-        def pv(i):
-            h, n, c, r, lo, noff = where(i)
+        def e_times_v(x):
+            h, n = tiles[x]
             a0 = 0 if n >= TPC else 1
             acc = ps_o.tile([P, D], F32)
-            st["acc", i] = acc
-            cod = st["cod", i]
-            scl = st["scl", i]
+            live["acc", x] = acc
+            cod = live["cod", x]
+            scl = live["scl", x]
             for a in range(a0, 2):
-                g = c - 1 + a
+                g = n // TPC - 1 + a
                 nc.tensor.matmul_mx(out=acc[:], lhsT=cod[:, a * P:(a + 1) * P].bitcast(FP8X4),
                                     lhsT_scale=scl[:, a * P:(a + 1) * P],
                                     rhs=v_cod[:, h, g * D:(g + 1) * D].bitcast(FP8X4),
                                     rhs_scale=v_scl[:, h, g * D:(g + 1) * D],
                                     start=(a == a0), stop=(a == 1))
 
-        def rsum(x):
-            if seq[x] % NT < TPC:
-                return
+        def add_row_sums(x):
             rsm = small.tile([P, 2], F32)
-            st["rsm", x // 2] = rsm
-            nc.vector.tensor_reduce(out=rsm[:], in_=st["rs", x // 2][:], axis=AX.X, op=ALU.add)
+            live["rsm", x] = rsm
+            nc.vector.tensor_reduce(out=rsm[:], in_=rs[:, x:x + 2, :], axis=AX.X, op=ALU.add)
 
-        def recip(x):
+        def invert_row_sums(x):
             rcp = small.tile([P, 2], F32)
-            st["rcp", x // 2] = rcp
-            if seq[x] % NT < TPC:
-                nc.vector.reciprocal(rcp[:], st["rs", x // 2][:, :, 0])
-            else:
-                nc.vector.reciprocal(rcp[:], st["rsm", x // 2][:])
+            live["rcp", x] = rcp
+            nc.vector.reciprocal(rcp[:], live["rsm", x][:])
 
-        def outp(x):
-            i = seq[x]
-            h, n, c, r, lo, noff = where(i)
+        def scale_and_store(x):
+            h, n = tiles[x]
             osb = opool.tile([P, D], F32)
-            nc.vector.tensor_scalar(out=osb[:], in0=st["acc", i][:], scalar1=st["rcp", x // 2][:, x % 2:x % 2 + 1],
-                                    scalar2=None, op0=ALU.mult)
+            rcp = live["rcp", x - x % 2]
+            nc.vector.tensor_scalar(out=osb[:], in0=live["acc", x][:], scalar1=rcp[:, x % 2:x % 2 + 1], scalar2=None,
+                                    op0=ALU.mult)
             nc.sync.dma_start(out=ov[h][:, n, :], in_=osb[:])
 
+        def stage(work, x, every=1):
+            if 0 <= x < NQ and x % every == 0:
+                work(x)
 
-        def stage(fn, x):
-            if 0 <= x < NQ:
-                fn(seq[x])
-
-        def stage_x(fn, x):
-            if 0 <= x < NQ:
-                fn(x)
-
-        prep_pe(0, 0)
-        prep_out(0, 0)
+        transpose_qk(0, 0)
+        copy_qk(0, 0)
+        diagonal_scores(0, 0)
         for g in range(NCH):
-            vprep(0, g)
-        vquant(0, 0)
-        vquant(0, 1)
+            regroup_v(0, g)
+        quantise_v(0, 0)
+        diagonal_max(0, 0)
+        quantise_v(0, 1)
         for s in range(-2, NQ + 4):
-            new_prep = s // 3 + 1 if s >= 0 and s % 3 == 0 and s // 3 + 1 < H * NCH else 0
-            nxt = s // TPC + 1 if s >= 0 and s // TPC + 1 < H * NCH and chunks[s // TPC + 1][1] > 0 else 0
-            stage(trans, s - 1)
-            stage(score_a, s + 2)
-            stage(pv, s - 3)
-            stage(score_b, s + 2)
-            if new_prep:
-                prep_pe(chunks[new_prep][0], chunks[new_prep][1])
-            if nxt and s % TPC == 1:
-                diag_pe(chunks[nxt][0], chunks[nxt][1])
-            if (s - 3) % 2 == 0:
-                stage_x(recip, s - 3)
-            stage(rowmax, s + 1)
-            stage(quant, s - 2)
-            stage(negmax, s + 1)
-            stage_x(outp, s - 3)
-            if (s - 2) % 2 == 0:
-                stage_x(rsum, s - 2)
-            stage_x(expo, s)
-            stage(evac_s, s - 1)
+            new_qk = chunks[s // 3 + 1] if s >= 0 and s % 3 == 0 and s // 3 + 1 < H * NCH else None
+            new_dg = chunks[s // TPC + 1] if s >= 0 and s % TPC == 1 and s // TPC + 1 < H * NCH else None
+            stage(transpose_e, s - 1)
+            stage(scores_unmasked, s + 2)
+            stage(e_times_v, s - 3)
+            stage(scores_masked, s + 2)
+            if new_qk:
+                transpose_qk(new_qk[0], new_qk[1])
+            if new_dg:
+                diagonal_scores(new_dg[0], new_dg[1])
+            stage(row_max, s + 1)
+            stage(invert_row_sums, s - 3, 2)
+            stage(quantise_e, s - 2)
+            stage(bias, s + 1)
+            stage(scale_and_store, s - 3)
+            stage(add_row_sums, s - 2, 2)
+            stage(exponentials, s)
+            stage(copy_e, s - 1)
             if 0 <= s < 2:
-                vquant(0, s + 2)
+                quantise_v(0, s + 2)
             if 2 * NCH <= s < 4 * NCH and s % 2 == 0:
-                vprep(chunks[s // 2][0], chunks[s // 2][1])
+                regroup_v(chunks[s // 2][0], chunks[s // 2][1])
             if 2 * NCH <= s < 4 * NCH and s % 2 == 1:
-                vquant(chunks[s // 2][0], chunks[s // 2][1])
-            if new_prep:
-                prep_out(chunks[new_prep][0], chunks[new_prep][1])
-            if nxt and s % TPC == 2:
-                diag_max(chunks[nxt][0], chunks[nxt][1])
+                quantise_v(chunks[s // 2][0], chunks[s // 2][1])
+            if new_qk:
+                copy_qk(new_qk[0], new_qk[1])
+            if new_dg:
+                diagonal_max(new_dg[0], new_dg[1])

from contextlib import ExitStack
import math

import concourse.mybir as mybir
from concourse.masks import make_identity

F32 = mybir.dt.float32
BF16 = mybir.dt.bfloat16
U32 = mybir.dt.uint32
U8 = mybir.dt.uint8
FP8X4 = mybir.dt.float8_e4m3fn_x4
ALU = mybir.AluOpType
ACT = mybir.ActivationFunctionType
AX = mybir.AxisListType

H, S, D, W = 2, 2048, 128, 512
P = 128
NT = S // P
TPC = W // P
NCH = S // W
NQ = H * NT
SCALE = 1.0 / math.sqrt(D)
MASKED = -17179869184.0
FLOPS = 2 * 2 * H * D * (W * W + (NCH - 1) * W * 2 * W)


def tile_multiheadattn_kernel(tc, q, k, v, layer_idx, out):
    assert layer_idx % 2 == 1, "only the local mask of the odd layers is built"
    nc = tc.nc
    qv = q.rearrange("b h (n p) d -> (b h) p n d", p=P)
    kv = k.rearrange("b h (n p) d -> (b h) p n d", p=P)
    vv = v.rearrange("b h (n p) d -> (b h) p n d", p=P)
    ov = out.rearrange("b h (n p) d -> (b h) p n d", p=P)

    tiles = [(0, n) for n in range(NT)] + [(1, n) for n in range(NT - 1, -1, -1)]
    chunks = [(0, c) for c in range(NCH)] + [(1, c) for c in range(NCH - 1, -1, -1)]

    with ExitStack() as ctx:
        keep = ctx.enter_context(tc.tile_pool(name="keep", bufs=1))
        small = ctx.enter_context(tc.tile_pool(name="small", bufs=10))
        epool = ctx.enter_context(tc.tile_pool(name="epool", bufs=3))
        cpool = ctx.enter_context(tc.tile_pool(name="cpool", bufs=3))
        opool = ctx.enter_context(tc.tile_pool(name="opool", bufs=4))
        ps_a = ctx.enter_context(tc.psum_pool(name="ps_a", bufs=3))
        ps_d = ctx.enter_context(tc.psum_pool(name="ps_d", bufs=2))
        ps_t = ctx.enter_context(tc.psum_pool(name="ps_t", bufs=2))
        ps_o = ctx.enter_context(tc.psum_pool(name="ps_o", bufs=1))
        ctx.enter_context(tc.manual_schedule())

        q_raw = keep.tile([P, H, NT, D], BF16)
        k_raw = keep.tile([P, H, NT, D], BF16)
        v_raw = keep.tile([P, H, NT, D], BF16)
        qkT = keep.tile([P, H, 2, S], BF16)
        v_grp = keep.tile([P, H, NCH, D, TPC], BF16, align_bytes=64)
        v_cod = keep.tile([P, H, NCH * D], U32, align_bytes=64)
        v_scl = keep.tile([P, H, NCH * D], U8, align_bytes=64)
        ident = keep.tile([P, P], BF16)
        mask_f = keep.tile([P, 2, P], F32)
        mask_b = keep.tile([P, 2, P], BF16)
        spread = keep.tile([P, 2, W], BF16)
        warm = keep.tile([P, 2], F32)
        rs = keep.tile([P, NQ, 2], F32)
        ge = []
        for r in range(TPC):
            ge_r = keep.tile([P, 2, P, TPC], BF16, name="ge%d" % r, align_bytes=64)
            ge.append(ge_r)

        def load(queue, raw, view, h, c):
            queue.dma_start(out=raw[:, h, c * TPC:(c + 1) * TPC, :], in_=view[h][:, c * TPC:(c + 1) * TPC, :])

        load(nc.sync, k_raw, kv, 0, 0)
        load(nc.scalar, q_raw, qv, 0, 0)
        for g in range(NCH):
            load(nc.sync, v_raw, vv, 0, g)
        for x, (h, c) in enumerate(chunks):
            if x > 0:
                load(nc.sync, k_raw, kv, h, c)
                load(nc.sync, q_raw, qv, h, c)
            if x == NCH:
                nc.sync.dma_start(out=v_raw[:, 1], in_=vv[1])

        make_identity(nc, ident[:])
        nc.vector.memset(warm[:, 0:1], 0.0)
        nc.scalar.activation(out=warm[:, 1:2], in_=warm[:, 0:1], func=ACT.Exp)
        nc.gpsimd.memset(mask_f[:], 0.0)
        nc.gpsimd.affine_select(out=mask_f[:, 0, :], in_=mask_f[:, 0, :], compare_op=ALU.is_ge, fill=MASKED,
                                base=0, pattern=[[-1, P]], channel_multiplier=1)
        nc.gpsimd.affine_select(out=mask_f[:, 1, :], in_=mask_f[:, 1, :], compare_op=ALU.is_ge, fill=MASKED,
                                base=-1, pattern=[[1, P]], channel_multiplier=-1)
        for r in range(1, TPC - 1):
            nc.vector.memset(ge[r][:], 0.0)
        nc.vector.memset(rs[:], 0.0)
        nc.vector.tensor_copy(out=mask_b[:], in_=mask_f[:])
        nc.gpsimd.memset(spread[:], 0.0)
        for y in range(2):
            nc.gpsimd.affine_select(out=spread[:, y, :], in_=spread[:, y, :], compare_op=ALU.not_equal, fill=1.0,
                                    base=3 * y, pattern=[[-1, W]], channel_multiplier=TPC)

        live = {}

        def transpose_qk(h, c):
            tp = ps_t.tile([P, 2 * TPC, P], BF16, tag="tp")
            live["tp", h, c] = tp
            for j in range(TPC):
                nc.tensor.transpose(tp[:, j, :], q_raw[:, h, c * TPC + j, :], ident[:])
            for j in range(TPC):
                nc.tensor.transpose(tp[:, TPC + j, :], k_raw[:, h, c * TPC + j, :], ident[:])

        def copy_qk(h, c):
            nc.vector.tensor_copy(out=qkT[:, h, :, c * W:(c + 1) * W],
                                  in_=live["tp", h, c][:].rearrange("p (a j) w -> p a (j w)", a=2))

        def regroup_v(h, g):
            dst = v_grp[:, h, g].rearrange("p (c i) t -> p c t i", i=4)
            src = v_raw[:, h, g * TPC:(g + 1) * TPC, :].rearrange("p t (c i) -> p c t i", i=4)
            if h == 0:
                nc.scalar.copy(out=dst, in_=src)
            else:
                nc.vector.tensor_copy(out=dst, in_=src)

        def quantise_v(h, g):
            nc.vector.quantize_mx(out=v_cod[:, h, g * D:(g + 1) * D].bitcast(FP8X4),
                                  scales=v_scl[:, h, g * D:(g + 1) * D],
                                  in_=v_grp[:, h, g].rearrange("p d t -> p (d t)"))

        def diagonal_scores(h, c):
            dg = ps_d.tile([P, TPC, P], F32)
            live["dg", h, c] = dg
            for r in range(TPC):
                n = c * TPC + r
                nc.tensor.matmul(dg[:, r, :], lhsT=ident[:], rhs=mask_b[:, 0, :], start=True, stop=False)
                nc.tensor.matmul(dg[:, r, :], lhsT=qkT[:, h, 0, n * P:(n + 1) * P],
                                 rhs=qkT[:, h, 1, n * P:(n + 1) * P], start=False, stop=True)

        def diagonal_max(h, c):
            rd = small.tile([P, TPC], F32)
            live["rd", h, c] = rd
            nc.vector.tensor_reduce(out=rd[:], in_=live["dg", h, c][:], axis=AX.X, op=ALU.max)

        def older(n):
            return min(n, TPC)

        def scores_unmasked(x):
            h, n = tiles[x]
            if n == 0:
                return
            sa = ps_a.tile([P, W], F32)
            live["sa", x] = sa
            first = 1 if n >= TPC else 0
            nc.tensor.matmul(sa[:, first * P:older(n) * P], lhsT=qkT[:, h, 0, n * P:(n + 1) * P],
                             rhs=qkT[:, h, 1, (n - older(n) + first) * P:n * P], start=True, stop=True)

        def scores_masked(x):
            h, n = tiles[x]
            if n < TPC:
                return
            sa = live["sa", x]
            nc.tensor.matmul(sa[:, 0:P], lhsT=ident[:], rhs=mask_b[:, 1, :], start=True, stop=False)
            nc.tensor.matmul(sa[:, 0:P], lhsT=qkT[:, h, 0, n * P:(n + 1) * P],
                             rhs=qkT[:, h, 1, (n - TPC) * P:(n - TPC + 1) * P], start=False, stop=True)

        def row_max(x):
            h, n = tiles[x]
            if n == 0:
                return
            r1 = small.tile([P, 1], F32)
            live["r1", x] = r1
            nc.vector.tensor_reduce(out=r1[:], in_=live["sa", x][:, 0:older(n) * P], axis=AX.X, op=ALU.max)

        def bias(x):
            h, n = tiles[x]
            rd = live["rd", h, n // TPC]
            nb = small.tile([P, 1], F32)
            live["nb", x] = nb
            if n == 0:
                nc.vector.tensor_scalar(out=nb[:], in0=rd[:, 0:1], scalar1=-SCALE, scalar2=None, op0=ALU.mult)
            else:
                nc.vector.tensor_scalar(out=nb[:], in0=live["r1", x][:], scalar1=rd[:, n % TPC:n % TPC + 1],
                                        scalar2=-SCALE, op0=ALU.max, op1=ALU.mult)

        def exponentials(x):
            h, n = tiles[x]
            e = epool.tile([P, (TPC + 1) * P], BF16)
            live["e", x] = e
            nb = live["nb", x]
            if n > 0:
                nc.scalar.activation(out=e[:, 0:older(n) * P], in_=live["sa", x][:, 0:older(n) * P], func=ACT.Exp,
                                     bias=nb[:], scale=SCALE, accum_out=rs[:, x, 0:1])
            nc.scalar.activation(out=e[:, older(n) * P:(older(n) + 1) * P], in_=live["dg", h, n // TPC][:, n % TPC, :],
                                 func=ACT.Exp, bias=nb[:], scale=SCALE, accum_out=rs[:, x, 1:2])

        def passes(n):
            u0 = n - older(n) - (n // TPC - 1) * TPC
            found = []
            for a in range(u0 // TPC, 2):
                u_lo = max(u0, a * TPC)
                u_hi = min(u0 + older(n) + 1, (a + 1) * TPC)
                found.append((a, u_lo - u0, u_hi - u_lo, u_lo - a * TPC))
            return found

        def transpose_e(x):
            h, n = tiles[x]
            et = ps_t.tile([P, 2 * TPC, P], BF16, tag="tp")
            live["et", x] = et
            e = live["e", x]
            filled = 0
            for a, j0, count, t0 in passes(n):
                if count == 1:
                    for m in range(TPC):
                        nc.tensor.transpose(et[:, TPC + m, :], e[:, j0 * P:(j0 + 1) * P],
                                            spread[:, t0 // 3, m * P:(m + 1) * P])
                else:
                    for j in range(j0, j0 + count):
                        nc.tensor.transpose(et[:, filled, :], e[:, j * P:(j + 1) * P], ident[:])
                        filled += 1

        def copy_e(x):
            h, n = tiles[x]
            et = live["et", x]
            done = 0
            for a, j0, count, t0 in passes(n):
                if count == 1:
                    nc.scalar.copy(out=ge[n % TPC][:, a].rearrange("p w t -> p (w t)"),
                                   in_=et[:, TPC:2 * TPC, :].rearrange("p t w -> p (t w)"))
                else:
                    nc.scalar.copy(out=ge[n % TPC][:, a, :, t0:t0 + count],
                                   in_=et[:, done:done + count, :].rearrange("p t w -> p w t"))
                    done += count

        def quantise_e(x):
            h, n = tiles[x]
            a0 = 0 if n >= TPC else 1
            cod = cpool.tile([P, 2 * P], U32, align_bytes=64)
            scl = cpool.tile([P, 2 * P], U8, align_bytes=64)
            live["cod", x] = cod
            live["scl", x] = scl
            nc.vector.quantize_mx(out=cod[:, a0 * P:2 * P].bitcast(FP8X4), scales=scl[:, a0 * P:2 * P],
                                  in_=ge[n % TPC][:, a0:2].rearrange("p a w t -> p (a w t)"))

        def e_times_v(x):
            h, n = tiles[x]
            a0 = 0 if n >= TPC else 1
            acc = ps_o.tile([P, D], F32)
            live["acc", x] = acc
            cod = live["cod", x]
            scl = live["scl", x]
            for a in range(a0, 2):
                g = n // TPC - 1 + a
                nc.tensor.matmul_mx(out=acc[:], lhsT=cod[:, a * P:(a + 1) * P].bitcast(FP8X4),
                                    lhsT_scale=scl[:, a * P:(a + 1) * P],
                                    rhs=v_cod[:, h, g * D:(g + 1) * D].bitcast(FP8X4),
                                    rhs_scale=v_scl[:, h, g * D:(g + 1) * D],
                                    start=(a == a0), stop=(a == 1))

        def add_row_sums(x):
            rsm = small.tile([P, 2], F32)
            live["rsm", x] = rsm
            nc.vector.tensor_reduce(out=rsm[:], in_=rs[:, x:x + 2, :], axis=AX.X, op=ALU.add)

        def invert_row_sums(x):
            rcp = small.tile([P, 2], F32)
            live["rcp", x] = rcp
            nc.vector.reciprocal(rcp[:], live["rsm", x][:])

        def scale_and_store(x):
            h, n = tiles[x]
            osb = opool.tile([P, D], F32)
            rcp = live["rcp", x - x % 2]
            nc.vector.tensor_scalar(out=osb[:], in0=live["acc", x][:], scalar1=rcp[:, x % 2:x % 2 + 1], scalar2=None,
                                    op0=ALU.mult)
            nc.sync.dma_start(out=ov[h][:, n, :], in_=osb[:])

        def stage(work, x, every=1):
            if 0 <= x < NQ and x % every == 0:
                work(x)

        transpose_qk(0, 0)
        copy_qk(0, 0)
        diagonal_scores(0, 0)
        for g in range(NCH):
            regroup_v(0, g)
        quantise_v(0, 0)
        diagonal_max(0, 0)
        quantise_v(0, 1)
        for s in range(-2, NQ + 4):
            new_qk = chunks[s // 3 + 1] if s >= 0 and s % 3 == 0 and s // 3 + 1 < H * NCH else None
            new_dg = chunks[s // TPC + 1] if s >= 0 and s % TPC == 1 and s // TPC + 1 < H * NCH else None
            stage(transpose_e, s - 1)
            stage(scores_unmasked, s + 2)
            stage(e_times_v, s - 3)
            stage(scores_masked, s + 2)
            if new_qk:
                transpose_qk(new_qk[0], new_qk[1])
            if new_dg:
                diagonal_scores(new_dg[0], new_dg[1])
            stage(row_max, s + 1)
            stage(invert_row_sums, s - 3, 2)
            stage(quantise_e, s - 2)
            stage(bias, s + 1)
            stage(scale_and_store, s - 3)
            stage(add_row_sums, s - 2, 2)
            stage(exponentials, s)
            stage(copy_e, s - 1)
            if 0 <= s < 2:
                quantise_v(0, s + 2)
            if 2 * NCH <= s < 4 * NCH and s % 2 == 0:
                regroup_v(chunks[s // 2][0], chunks[s // 2][1])
            if 2 * NCH <= s < 4 * NCH and s % 2 == 1:
                quantise_v(chunks[s // 2][0], chunks[s // 2][1])
            if new_qk:
                copy_qk(new_qk[0], new_qk[1])
            if new_dg:
                diagonal_max(new_dg[0], new_dg[1])
